import numpy as np
import ml_dtypes


def mxq(x, axis, fmt="e4m3"):
    dtype, down = {"e4m3": (ml_dtypes.float8_e4m3fn, 7), "e5m2": (ml_dtypes.float8_e5m2, 14)}[fmt]
    v = np.moveaxis(np.asarray(x, np.float32).astype(ml_dtypes.bfloat16).astype(np.float64), axis, -1)
    blocks = v.reshape(v.shape[:-1] + (-1, 32))
    amax = np.abs(blocks).max(-1, keepdims=True)
    byte = np.maximum(np.where(amax > 0, np.frexp(amax)[1] - 1 + 127, 0) - down, 1)
    scale = np.exp2(byte - 127.0)
    codes = (blocks / scale).astype(np.float32).astype(dtype).astype(np.float64)
    return np.moveaxis((codes * scale).reshape(v.shape), -1, axis)


WIDE = False


def mx_kscale(k):
    if not WIDE:
        return np.ones(k)
    levels = np.array([10, -10, 5, -5, 0])
    a = np.random.permutation(np.resize(levels, k // 512 * 4)).reshape(k // 512, 4)
    idx = np.arange(k)
    return np.exp2(a[idx // 512, idx % 128 // 32])


BF16 = ml_dtypes.bfloat16


def bf(x):
    return np.asarray(x, np.float32).astype(BF16)


def f64(x):
    return np.asarray(x).astype(np.float64)


P, N, Z, H1, H2, C = 8, 256, 16, 512, 2048, 256
EPS = 1e-5


def batch_norm(h, gamma, beta):
    mu = h.mean(axis=1, keepdims=True)
    var = h.var(axis=1, keepdims=True)
    return (h - mu) * (1.0 / np.sqrt(var + EPS)) * gamma[:, None, :] + beta[:, None, :]


def setup_inputs():
    r = np.random.standard_normal
    t = mx_kscale(H2)
    sd = np.where(np.random.random((P, 1, H2)) < 0.25, np.sqrt(EPS), 1.0)
    return {"h7_pre": bf((r((P, N, H2)) + 0.5 * r((P, 1, H2))) * sd),
            "g7": bf((1.0 + 0.1 * r((P, H2))) * t),
            "be7": bf(0.3 * r((P, H2)) * t),
            "W8": bf(1.5 * r((P, C, H2)) / np.sqrt(H2) / t),
            "b8": bf(0.5 * r((P, C)))}


def reference(h7_pre, g7, be7, W8, b8):
    a = np.maximum(batch_norm(f64(h7_pre), f64(g7), f64(be7)), 0.0)
    y = (mxq(a, 2, "e4m3") @ mxq(f64(W8), 2, "e4m3").transpose(0, 2, 1)) + f64(b8)[:, None, :]
    em = 1.0 / (1.0 + np.exp(-y))
    return em.transpose(1, 0, 2)

@@ -1,0 +1,247 @@
+from contextlib import ExitStack
+
+import concourse.mybir as mybir
+from concourse.masks import make_identity
+
+F32 = mybir.dt.float32
+BF16 = mybir.dt.bfloat16
+U32 = mybir.dt.uint32
+U8 = mybir.dt.uint8
+FP8X4 = mybir.dt.float8_e4m3fn_x4
+ALU = mybir.AluOpType
+ACT = mybir.ActivationFunctionType
+
+NBLK, ROWS, K, CH = 8, 256, 2048, 256
+EPS = 1e-5
+P = 128
+PASSES = K // 512
+STEPS = NBLK * PASSES
+FLOPS = 2 * NBLK * ROWS * CH * K
+
+D_W = 4
+D_B = 6
+RG_ENGINE = "v"
+
+
+def tile_decoder_pb_kernel(tc, h7_pre, g7, be7, W8, b8, out):
+    nc = tc.nc
+    with ExitStack() as ctx:
+        const = ctx.enter_context(tc.tile_pool(name="const", bufs=1))
+        resident = ctx.enter_context(tc.tile_pool(name="resident", bufs=NBLK))
+        small = ctx.enter_context(tc.tile_pool(name="small", bufs=2))
+        work = ctx.enter_context(tc.tile_pool(name="work", bufs=3))
+        codes = ctx.enter_context(tc.tile_pool(name="codes", bufs=2))
+        psum = ctx.enter_context(tc.psum_pool(name="psum", bufs=2))
+        ctx.enter_context(tc.manual_schedule())
+
+        hx = []
+        wx = []
+        for p in range(NBLK):
+            hx_p = resident.tile([P, 2 * K], BF16, name="hx_p", tag="hx")
+            wx_p = resident.tile([P, 2 * K], BF16, name="wx_p", tag="wx")
+            hx.append(hx_p)
+            wx.append(wx_p)
+
+        def load(dst, src, k0, k1):
+            nc.sync.dma_start(
+                out=dst[:].rearrange("n (t k) -> n t k", t=2)[:, :, k0:k1],
+                in_=src.rearrange("(t n) k -> n t k", t=2)[:, :, k0:k1],
+            )
+
+        gb_raw = const.tile([P, 256], BF16)
+        nc.scalar.dma_start(out=gb_raw[0:64, :], in_=g7.rearrange("p (r k) -> (p r) k", k=256))
+        nc.scalar.dma_start(out=gb_raw[64:128, :], in_=be7.rearrange("p (r k) -> (p r) k", k=256))
+        bb = const.tile([P, NBLK * CH], BF16)
+
+        for g in range(PASSES):
+            load(hx[0], h7_pre[0], g * 512, (g + 1) * 512)
+        load(hx[1], h7_pre[1], 0, K)
+        for p in range(NBLK):
+            load(wx[p], W8[p], 0, K)
+            if p == 1:
+                nc.sync.dma_start(out=bb[:], in_=b8.rearrange("p c -> (p c)").partition_broadcast(P))
+            if p + 2 < NBLK:
+                load(hx[p + 2], h7_pre[p + 2], 0, K)
+
+        ident = const.tile([P, P], F32)
+        make_identity(nc, ident[:])
+        neg_half = const.tile([P, 16], F32)
+        nc.gpsimd.memset(neg_half[:], -0.5)
+        warm = const.tile([P, 1], F32)
+        nc.vector.memset(warm[:], 0.0)
+        nc.scalar.activation(out=warm[:], in_=warm[:], func=ACT.Sigmoid)
+
+        gb_t = psum.tile([P, 512], F32, name="gb_t", tag="wt")
+        nc.tensor.transpose(gb_t[:, 0:P], gb_raw[:].bitcast(F32), ident[:])
+        gb = const.tile([P, 256], F32)
+        nc.vector.tensor_copy(out=gb[:], in_=gb_t[:, 0:P].bitcast(BF16))
+
+        st = const.tile([P, NBLK * 8 * 6], F32)
+        sc = const.tile([P, NBLK * 16], F32)
+        bi = const.tile([P, NBLK * 16], F32)
+        out_v = out.rearrange("(t n) p c -> n t p c", t=2)
+
+        def transposes(bank, src, g):
+            words = src[:].bitcast(F32)
+            for u in range(2):
+                for t in range(2):
+                    nc.tensor.transpose(
+                        bank[:, u * 256 + t * P : u * 256 + (t + 1) * P],
+                        words[:, t * 1024 + (2 * g + u) * P : t * 1024 + (2 * g + u + 1) * P],
+                        ident[:],
+                    )
+
+        def chain(p):
+            stp = st[:, p * 48 : (p + 1) * 48].rearrange("q (c s) -> q c s", s=3)
+            cols = slice(p * 16, (p + 1) * 16)
+            var = small.tile([P, 16], F32, name="var", tag="var")
+            nc.gpsimd.tensor_scalar(
+                out=var[:], in0=stp[:, :, 2], scalar1=1.0 / ROWS, scalar2=EPS, op0=ALU.mult, op1=ALU.add
+            )
+            rstd = small.tile([P, 16], F32, name="rstd", tag="rstd")
+            nc.gpsimd.tensor_tensor(out=rstd[:], in0=var[:], in1=neg_half[:], op=ALU.pow)
+            nc.gpsimd.tensor_tensor(out=sc[:, cols], in0=rstd[:], in1=gb[:, cols], op=ALU.mult)
+            ms = small.tile([P, 16], F32, name="ms", tag="ms")
+            nc.gpsimd.tensor_tensor(out=ms[:], in0=stp[:, :, 1], in1=sc[:, cols], op=ALU.mult)
+            nc.gpsimd.tensor_tensor(
+                out=bi[:, cols], in0=gb[:, 128 + p * 16 : 128 + (p + 1) * 16], in1=ms[:], op=ALU.subtract
+            )
+
+        banks = {}
+        tiles = {}
+
+        def regroup(s):
+            planes = tiles[("planes", s)]
+            grouped = work.tile([P, 4 * ROWS], BF16, name="grouped", tag="grouped", align_bytes=64)
+            tiles[("grouped", s)] = grouped
+            eng = RG_ENGINE[s % len(RG_ENGINE)]
+            dst = grouped[:].rearrange("q (c i j) -> q c j i", i=4, j=4)
+            src = planes[:].rearrange("q (j c i) -> q c j i", i=4, j=4)
+            if eng == "v":
+                nc.vector.tensor_copy(out=dst, in_=src)
+            elif eng == "s":
+                nc.scalar.copy(out=dst, in_=src)
+            else:
+                nc.gpsimd.tensor_scalar(out=dst, in0=src, scalar1=1.0, scalar2=0.0, op0=ALU.mult, op1=ALU.add)
+
+        def product(p):
+            ac, asc = tiles[("ac", p)]
+            wc, ws = tiles[("wc", p)]
+            acc = psum.tile([P, 512], F32, name="acc", tag="acc")
+            banks[("acc", p)] = acc
+            for t in range(2):
+                for g in range(PASSES):
+                    a_cols = slice(g * ROWS + t * P, g * ROWS + (t + 1) * P)
+                    w_cols = slice(g * CH, (g + 1) * CH)
+                    nc.tensor.matmul_mx(
+                        out=acc[:, t * CH : (t + 1) * CH],
+                        lhsT=ac[:, a_cols].bitcast(FP8X4),
+                        lhsT_scale=asc[:, a_cols],
+                        rhs=wc[:, w_cols].bitcast(FP8X4),
+                        rhs_scale=ws[:, w_cols],
+                        start=(g == 0),
+                        stop=(g == PASSES - 1),
+                    )
+
+        def add_bias(p):
+            acc = banks[("acc", p)]
+            y = work.tile([P, 2 * CH], F32, name="y", tag="y")
+            tiles[("y", p)] = y
+            nc.vector.tensor_tensor(
+                out=y[:].rearrange("n (t c) -> n t c", t=2),
+                in0=acc[:].rearrange("n (t c) -> n t c", t=2),
+                in1=bb[:, p * CH : (p + 1) * CH].unsqueeze(1).to_broadcast([P, 2, CH]),
+                op=ALU.add,
+            )
+
+        def sigmoid_store(p):
+            y = tiles[("y", p)]
+            o = work.tile([P, 2 * CH], F32, name="o", tag="o")
+            nc.scalar.activation(out=o[:], in_=y[:], func=ACT.Sigmoid)
+            nc.sync.dma_start(out=out_v[:, :, p, :], in_=o[:].rearrange("n (t c) -> n t c", t=2))
+
+        add_at = {}
+        sig_at = {}
+        for tau in range(STEPS + D_B + 6):
+            s_a, s_w, s_b = tau, tau - D_W, tau - D_B
+            if 0 <= s_b < STEPS:
+                hb = psum.tile([P, 512], F32, name="hb", tag="hb")
+                banks[("hb", s_b)] = hb
+                transposes(hb, hx[s_b // PASSES], s_b % PASSES)
+            if 0 <= s_w < STEPS:
+                wt = psum.tile([P, 512], F32, name="wt", tag="wt")
+                banks[("wt", s_w)] = wt
+                transposes(wt, wx[s_w // PASSES], s_w % PASSES)
+            if s_a < STEPS:
+                ha = psum.tile([P, 512], F32, name="ha", tag="ha")
+                transposes(ha, hx[s_a // PASSES], s_a % PASSES)
+                hab = ha[:].bitcast(BF16)
+            if tau in add_at:
+                add_bias(add_at[tau])
+            if s_a < STEPS:
+                for u in range(2):
+                    col = 2 * s_a + u
+                    nc.vector.bn_stats(out=st[:, col * 6 : (col + 1) * 6], in_=hab[:, u * 512 : (u + 1) * 512])
+                if s_a % PASSES == PASSES - 1:
+                    chain(s_a // PASSES)
+            if tau in sig_at:
+                sigmoid_store(sig_at[tau])
+            if 0 <= s_b < STEPS:
+                hbb = banks[("hb", s_b)][:].bitcast(BF16).rearrange("q (u n e) -> q u n e", u=2, e=2)
+                planes = work.tile([P, 4 * ROWS], BF16, name="planes", tag="planes")
+                tiles[("planes", s_b)] = planes
+                for u in range(2):
+                    for e in range(2):
+                        col = (2 * s_b + u) * 2 + e
+                        j = 2 * u + e
+                        nc.scalar.activation(
+                            out=planes[:, j * ROWS : (j + 1) * ROWS],
+                            in_=hbb[:, u, :, e],
+                            func=ACT.Relu,
+                            bias=bi[:, col : col + 1],
+                            scale=sc[:, col : col + 1],
+                        )
+            if 0 <= s_w < STEPS:
+                wg = work.tile([P, 4 * CH], BF16, name="wg", tag="wg", align_bytes=64)
+                tiles[("wg", s_w)] = wg
+                nc.scalar.copy(
+                    out=wg[:].bitcast(F32).rearrange("q (c u) -> q c u", u=2),
+                    in_=banks[("wt", s_w)][:].rearrange("q (u c) -> q c u", u=2),
+                )
+            s_q = s_w - 1
+            if 0 <= s_q < STEPS:
+                p, g = s_q // PASSES, s_q % PASSES
+                if g == 0:
+                    wc = codes.tile([P, PASSES * CH], U32, name="wc", tag="wc", align_bytes=64)
+                    ws = codes.tile([P, PASSES * CH], U8, name="ws", tag="ws", align_bytes=64)
+                    tiles[("wc", p)] = (wc, ws)
+                wc, ws = tiles[("wc", p)]
+                nc.vector.quantize_mx(
+                    out=wc[:, g * CH : (g + 1) * CH].bitcast(FP8X4),
+                    scales=ws[:, g * CH : (g + 1) * CH],
+                    in_=tiles[("wg", s_q)][:],
+                )
+            s_q = s_b - 2
+            if 0 <= s_q < STEPS:
+                p, g = s_q // PASSES, s_q % PASSES
+                if g == 0:
+                    ac = codes.tile([P, PASSES * ROWS], U32, name="ac", tag="ac", align_bytes=64)
+                    asc = codes.tile([P, PASSES * ROWS], U8, name="asc", tag="asc", align_bytes=64)
+                    tiles[("ac", p)] = (ac, asc)
+                ac, asc = tiles[("ac", p)]
+                nc.vector.quantize_mx(
+                    out=ac[:, g * ROWS : (g + 1) * ROWS].bitcast(FP8X4),
+                    scales=asc[:, g * ROWS : (g + 1) * ROWS],
+                    in_=tiles[("grouped", s_q)][:],
+                )
+            if 0 <= s_b - 1 < STEPS:
+                regroup(s_b - 1)
+            if 0 <= s_q < STEPS and s_q % PASSES == PASSES - 1:
+                p = s_q // PASSES
+                product(p)
+                if p == NBLK - 1:
+                    add_bias(p)
+                    sigmoid_store(p)
+                else:
+                    add_at[tau + 1] = p
+                    sig_at[tau + 2] = p

@@ -18,9 +18,18 @@ PASSES = K // 512
 STEPS = NBLK * PASSES
 FLOPS = 2 * NBLK * ROWS * CH * K
 
-D_W = 4
-D_B = 6
-RG_ENGINE = "v"
+D_W = 2
+D_B = 4
+D_MX = 2
+UNIT = 2
+
+
+def regroup_engine(s):
+    return "s" if s % 4 == 3 else "v"
+
+
+def weights_copy_on_vector(s):
+    return s >= 30
 
 
 def tile_decoder_pb_kernel(tc, h7_pre, g7, be7, W8, b8, out):
@@ -29,7 +38,7 @@ def tile_decoder_pb_kernel(tc, h7_pre, g7, be7, W8, b8, out):
         const = ctx.enter_context(tc.tile_pool(name="const", bufs=1))
         resident = ctx.enter_context(tc.tile_pool(name="resident", bufs=NBLK))
         small = ctx.enter_context(tc.tile_pool(name="small", bufs=2))
-        work = ctx.enter_context(tc.tile_pool(name="work", bufs=3))
+        work = ctx.enter_context(tc.tile_pool(name="work", bufs=4))
         codes = ctx.enter_context(tc.tile_pool(name="codes", bufs=2))
         psum = ctx.enter_context(tc.psum_pool(name="psum", bufs=2))
         ctx.enter_context(tc.manual_schedule())
@@ -53,19 +62,20 @@ def tile_decoder_pb_kernel(tc, h7_pre, g7, be7, W8, b8, out):
         nc.scalar.dma_start(out=gb_raw[64:128, :], in_=be7.rearrange("p (r k) -> (p r) k", k=256))
         bb = const.tile([P, NBLK * CH], BF16)
 
-        for g in range(PASSES):
-            load(hx[0], h7_pre[0], g * 512, (g + 1) * 512)
-        load(hx[1], h7_pre[1], 0, K)
-        for p in range(NBLK):
+        load(hx[0], h7_pre[0], 0, 512)
+        load(hx[0], h7_pre[0], 512, 1024)
+        load(wx[0], W8[0], 0, 1024)
+        load(hx[0], h7_pre[0], 1024, 2048)
+        load(wx[0], W8[0], 1024, 2048)
+        for p in range(1, NBLK):
+            load(hx[p], h7_pre[p], 0, K)
             load(wx[p], W8[p], 0, K)
             if p == 1:
                 nc.sync.dma_start(out=bb[:], in_=b8.rearrange("p c -> (p c)").partition_broadcast(P))
-            if p + 2 < NBLK:
-                load(hx[p + 2], h7_pre[p + 2], 0, K)
 
         ident = const.tile([P, P], F32)
         make_identity(nc, ident[:])
-        neg_half = const.tile([P, 16], F32)
+        neg_half = const.tile([P, 4 * UNIT], F32)
         nc.gpsimd.memset(neg_half[:], -0.5)
         warm = const.tile([P, 1], F32)
         nc.vector.memset(warm[:], 0.0)
@@ -91,20 +101,21 @@ def tile_decoder_pb_kernel(tc, h7_pre, g7, be7, W8, b8, out):
                         ident[:],
                     )
 
-        def chain(p):
-            stp = st[:, p * 48 : (p + 1) * 48].rearrange("q (c s) -> q c s", s=3)
-            cols = slice(p * 16, (p + 1) * 16)
-            var = small.tile([P, 16], F32, name="var", tag="var")
+        def chain(j):
+            w = 4 * UNIT
+            stp = st[:, j * 3 * w : (j + 1) * 3 * w].rearrange("q (c s) -> q c s", s=3)
+            cols = slice(j * w, (j + 1) * w)
+            var = small.tile([P, w], F32, name="var", tag="var")
             nc.gpsimd.tensor_scalar(
                 out=var[:], in0=stp[:, :, 2], scalar1=1.0 / ROWS, scalar2=EPS, op0=ALU.mult, op1=ALU.add
             )
-            rstd = small.tile([P, 16], F32, name="rstd", tag="rstd")
+            rstd = small.tile([P, w], F32, name="rstd", tag="rstd")
             nc.gpsimd.tensor_tensor(out=rstd[:], in0=var[:], in1=neg_half[:], op=ALU.pow)
             nc.gpsimd.tensor_tensor(out=sc[:, cols], in0=rstd[:], in1=gb[:, cols], op=ALU.mult)
-            ms = small.tile([P, 16], F32, name="ms", tag="ms")
+            ms = small.tile([P, w], F32, name="ms", tag="ms")
             nc.gpsimd.tensor_tensor(out=ms[:], in0=stp[:, :, 1], in1=sc[:, cols], op=ALU.mult)
             nc.gpsimd.tensor_tensor(
-                out=bi[:, cols], in0=gb[:, 128 + p * 16 : 128 + (p + 1) * 16], in1=ms[:], op=ALU.subtract
+                out=bi[:, cols], in0=gb[:, 128 + j * w : 128 + (j + 1) * w], in1=ms[:], op=ALU.subtract
             )
 
         banks = {}
@@ -114,7 +125,7 @@ def tile_decoder_pb_kernel(tc, h7_pre, g7, be7, W8, b8, out):
             planes = tiles[("planes", s)]
             grouped = work.tile([P, 4 * ROWS], BF16, name="grouped", tag="grouped", align_bytes=64)
             tiles[("grouped", s)] = grouped
-            eng = RG_ENGINE[s % len(RG_ENGINE)]
+            eng = regroup_engine(s)
             dst = grouped[:].rearrange("q (c i j) -> q c j i", i=4, j=4)
             src = planes[:].rearrange("q (j c i) -> q c j i", i=4, j=4)
             if eng == "v":
@@ -160,30 +171,30 @@ def tile_decoder_pb_kernel(tc, h7_pre, g7, be7, W8, b8, out):
             nc.scalar.activation(out=o[:], in_=y[:], func=ACT.Sigmoid)
             nc.sync.dma_start(out=out_v[:, :, p, :], in_=o[:].rearrange("n (t c) -> n t c", t=2))
 
+        mx_at = {}
         add_at = {}
         sig_at = {}
-        for tau in range(STEPS + D_B + 6):
+        for tau in range(STEPS + D_B + 8):
             s_a, s_w, s_b = tau, tau - D_W, tau - D_B
-            if 0 <= s_b < STEPS:
-                hb = psum.tile([P, 512], F32, name="hb", tag="hb")
-                banks[("hb", s_b)] = hb
-                transposes(hb, hx[s_b // PASSES], s_b % PASSES)
+            if s_a < STEPS:
+                hb = psum.tile([P, 512], F32, name="hb", tag="hb", bufs=4)
+                banks[("hb", s_a)] = hb
+                transposes(hb, hx[s_a // PASSES], s_a % PASSES)
             if 0 <= s_w < STEPS:
                 wt = psum.tile([P, 512], F32, name="wt", tag="wt")
                 banks[("wt", s_w)] = wt
                 transposes(wt, wx[s_w // PASSES], s_w % PASSES)
-            if s_a < STEPS:
-                ha = psum.tile([P, 512], F32, name="ha", tag="ha")
-                transposes(ha, hx[s_a // PASSES], s_a % PASSES)
-                hab = ha[:].bitcast(BF16)
+            if tau in mx_at:
+                product(mx_at[tau])
             if tau in add_at:
                 add_bias(add_at[tau])
             if s_a < STEPS:
+                hab = banks[("hb", s_a)][:].bitcast(BF16)
                 for u in range(2):
                     col = 2 * s_a + u
                     nc.vector.bn_stats(out=st[:, col * 6 : (col + 1) * 6], in_=hab[:, u * 512 : (u + 1) * 512])
-                if s_a % PASSES == PASSES - 1:
-                    chain(s_a // PASSES)
+                if s_a % UNIT == UNIT - 1:
+                    chain(s_a // UNIT)
             if tau in sig_at:
                 sigmoid_store(sig_at[tau])
             if 0 <= s_b < STEPS:
@@ -204,10 +215,12 @@ def tile_decoder_pb_kernel(tc, h7_pre, g7, be7, W8, b8, out):
             if 0 <= s_w < STEPS:
                 wg = work.tile([P, 4 * CH], BF16, name="wg", tag="wg", align_bytes=64)
                 tiles[("wg", s_w)] = wg
-                nc.scalar.copy(
-                    out=wg[:].bitcast(F32).rearrange("q (c u) -> q c u", u=2),
-                    in_=banks[("wt", s_w)][:].rearrange("q (u c) -> q c u", u=2),
-                )
+                wg_dst = wg[:].bitcast(F32).rearrange("q (c u) -> q c u", u=2)
+                wt_src = banks[("wt", s_w)][:].rearrange("q (u c) -> q c u", u=2)
+                if weights_copy_on_vector(s_w):
+                    nc.vector.tensor_copy(out=wg_dst, in_=wt_src)
+                else:
+                    nc.scalar.copy(out=wg_dst, in_=wt_src)
             s_q = s_w - 1
             if 0 <= s_q < STEPS:
                 p, g = s_q // PASSES, s_q % PASSES
@@ -238,10 +251,11 @@ def tile_decoder_pb_kernel(tc, h7_pre, g7, be7, W8, b8, out):
                 regroup(s_b - 1)
             if 0 <= s_q < STEPS and s_q % PASSES == PASSES - 1:
                 p = s_q // PASSES
-                product(p)
                 if p == NBLK - 1:
+                    product(p)
                     add_bias(p)
                     sigmoid_store(p)
                 else:
-                    add_at[tau + 1] = p
-                    sig_at[tau + 2] = p
+                    mx_at[tau + D_MX] = p
+                    add_at[tau + D_MX + 1] = p
+                    sig_at[tau + D_MX + 2] = p

@@ -18,9 +18,9 @@ PASSES = K // 512
 STEPS = NBLK * PASSES
 FLOPS = 2 * NBLK * ROWS * CH * K
 
-D_W = 2
-D_B = 4
-D_MX = 2
+D_W = 3
+D_B = 3
+D_MX = 3
 UNIT = 2
 
 
@@ -29,7 +29,7 @@ def regroup_engine(s):
 
 
 def weights_copy_on_vector(s):
-    return s >= 30
+    return s >= 28
 
 
 def tile_decoder_pb_kernel(tc, h7_pre, g7, be7, W8, b8, out):
@@ -138,7 +138,7 @@ def tile_decoder_pb_kernel(tc, h7_pre, g7, be7, W8, b8, out):
         def product(p):
             ac, asc = tiles[("ac", p)]
             wc, ws = tiles[("wc", p)]
-            acc = psum.tile([P, 512], F32, name="acc", tag="acc")
+            acc = psum.tile([P, 512], F32, name="acc", tag="acc", bufs=1)
             banks[("acc", p)] = acc
             for t in range(2):
                 for g in range(PASSES):
@@ -177,7 +177,7 @@ def tile_decoder_pb_kernel(tc, h7_pre, g7, be7, W8, b8, out):
         for tau in range(STEPS + D_B + 8):
             s_a, s_w, s_b = tau, tau - D_W, tau - D_B
             if s_a < STEPS:
-                hb = psum.tile([P, 512], F32, name="hb", tag="hb", bufs=4)
+                hb = psum.tile([P, 512], F32, name="hb", tag="hb", bufs=5)
                 banks[("hb", s_a)] = hb
                 transposes(hb, hx[s_a // PASSES], s_a % PASSES)
             if 0 <= s_w < STEPS:

@@ -18,14 +18,15 @@ PASSES = K // 512
 STEPS = NBLK * PASSES
 FLOPS = 2 * NBLK * ROWS * CH * K
 
-D_W = 3
-D_B = 3
-D_MX = 3
+D_W = 4
+D_B = 5
+D_MX = 2
+D_C = 3
 UNIT = 2
 
 
 def regroup_engine(s):
-    return "s" if s % 4 == 3 else "v"
+    return "s" if s % 3 == 2 else "v"
 
 
 def weights_copy_on_vector(s):
@@ -81,7 +82,7 @@ def tile_decoder_pb_kernel(tc, h7_pre, g7, be7, W8, b8, out):
         nc.vector.memset(warm[:], 0.0)
         nc.scalar.activation(out=warm[:], in_=warm[:], func=ACT.Sigmoid)
 
-        gb_t = psum.tile([P, 512], F32, name="gb_t", tag="wt")
+        gb_t = psum.tile([P, 512], F32, name="gb_t", tag="wt", bufs=1)
         nc.tensor.transpose(gb_t[:, 0:P], gb_raw[:].bitcast(F32), ident[:])
         gb = const.tile([P, 256], F32)
         nc.vector.tensor_copy(out=gb[:], in_=gb_t[:, 0:P].bitcast(BF16))
@@ -101,22 +102,31 @@ def tile_decoder_pb_kernel(tc, h7_pre, g7, be7, W8, b8, out):
                         ident[:],
                     )
 
-        def chain(j):
+        def chain_pool(j):
             w = 4 * UNIT
             stp = st[:, j * 3 * w : (j + 1) * 3 * w].rearrange("q (c s) -> q c s", s=3)
-            cols = slice(j * w, (j + 1) * w)
             var = small.tile([P, w], F32, name="var", tag="var")
             nc.gpsimd.tensor_scalar(
                 out=var[:], in0=stp[:, :, 2], scalar1=1.0 / ROWS, scalar2=EPS, op0=ALU.mult, op1=ALU.add
             )
-            rstd = small.tile([P, w], F32, name="rstd", tag="rstd")
+            rstd = small.tile([P, w], F32, name="rstd", tag="rstd", bufs=4)
+            tiles[("rstd", j)] = rstd
             nc.gpsimd.tensor_tensor(out=rstd[:], in0=var[:], in1=neg_half[:], op=ALU.pow)
-            nc.gpsimd.tensor_tensor(out=sc[:, cols], in0=rstd[:], in1=gb[:, cols], op=ALU.mult)
-            ms = small.tile([P, w], F32, name="ms", tag="ms")
-            nc.gpsimd.tensor_tensor(out=ms[:], in0=stp[:, :, 1], in1=sc[:, cols], op=ALU.mult)
-            nc.gpsimd.tensor_tensor(
-                out=bi[:, cols], in0=gb[:, 128 + j * w : 128 + (j + 1) * w], in1=ms[:], op=ALU.subtract
-            )
+
+        def chain_vector(j, part):
+            w = 4 * UNIT
+            stp = st[:, j * 3 * w : (j + 1) * 3 * w].rearrange("q (c s) -> q c s", s=3)
+            cols = slice(j * w, (j + 1) * w)
+            if part == 0:
+                nc.vector.tensor_tensor(out=sc[:, cols], in0=tiles[("rstd", j)][:], in1=gb[:, cols], op=ALU.mult)
+            elif part == 1:
+                ms = small.tile([P, w], F32, name="ms", tag="ms")
+                tiles[("ms", j)] = ms
+                nc.vector.tensor_tensor(out=ms[:], in0=stp[:, :, 1], in1=sc[:, cols], op=ALU.mult)
+            else:
+                nc.vector.tensor_tensor(
+                    out=bi[:, cols], in0=gb[:, 128 + j * w : 128 + (j + 1) * w], in1=tiles[("ms", j)][:], op=ALU.subtract
+                )
 
         banks = {}
         tiles = {}
@@ -177,24 +187,32 @@ def tile_decoder_pb_kernel(tc, h7_pre, g7, be7, W8, b8, out):
         for tau in range(STEPS + D_B + 8):
             s_a, s_w, s_b = tau, tau - D_W, tau - D_B
             if s_a < STEPS:
-                hb = psum.tile([P, 512], F32, name="hb", tag="hb", bufs=5)
+                hb = psum.tile([P, 512], F32, name="hb", tag="hb", bufs=6)
                 banks[("hb", s_a)] = hb
                 transposes(hb, hx[s_a // PASSES], s_a % PASSES)
             if 0 <= s_w < STEPS:
-                wt = psum.tile([P, 512], F32, name="wt", tag="wt")
+                wt = psum.tile([P, 512], F32, name="wt", tag="wt", bufs=1)
                 banks[("wt", s_w)] = wt
                 transposes(wt, wx[s_w // PASSES], s_w % PASSES)
             if tau in mx_at:
                 product(mx_at[tau])
             if tau in add_at:
                 add_bias(add_at[tau])
+            j_c = (tau - D_C - (UNIT - 1)) // UNIT if (tau - D_C - (UNIT - 1)) % UNIT == 0 else -1
+            do_chain = 0 <= j_c < STEPS // UNIT
+            if do_chain:
+                chain_vector(j_c, 0)
             if s_a < STEPS:
                 hab = banks[("hb", s_a)][:].bitcast(BF16)
-                for u in range(2):
-                    col = 2 * s_a + u
-                    nc.vector.bn_stats(out=st[:, col * 6 : (col + 1) * 6], in_=hab[:, u * 512 : (u + 1) * 512])
+                nc.vector.bn_stats(out=st[:, 2 * s_a * 6 : (2 * s_a + 1) * 6], in_=hab[:, 0:512])
+            if do_chain:
+                chain_vector(j_c, 1)
+            if s_a < STEPS:
+                nc.vector.bn_stats(out=st[:, (2 * s_a + 1) * 6 : (2 * s_a + 2) * 6], in_=hab[:, 512:1024])
                 if s_a % UNIT == UNIT - 1:
-                    chain(s_a // UNIT)
+                    chain_pool(s_a // UNIT)
+            if do_chain:
+                chain_vector(j_c, 2)
             if tau in sig_at:
                 sigmoid_store(sig_at[tau])
             if 0 <= s_b < STEPS:

@@ -18,19 +18,17 @@ PASSES = K // 512
 STEPS = NBLK * PASSES
 FLOPS = 2 * NBLK * ROWS * CH * K
 
-D_W = 4
-D_B = 5
-D_MX = 2
-D_C = 3
 UNIT = 2
+N_UNITS = STEPS // UNIT
+LAG_W = 1
+LAG_CHAIN = 3
+LAG_NORM = 5
+LAG_MX = 2
+H_BANKS = 6
 
 
-def regroup_engine(s):
-    return "s" if s % 3 == 2 else "v"
-
-
-def weights_copy_on_vector(s):
-    return s >= 28
+def regroup_on_scalar(s):
+    return s % 3 == 2 and s < 24
 
 
 def tile_decoder_pb_kernel(tc, h7_pre, g7, be7, W8, b8, out):
@@ -38,10 +36,10 @@ def tile_decoder_pb_kernel(tc, h7_pre, g7, be7, W8, b8, out):
     with ExitStack() as ctx:
         const = ctx.enter_context(tc.tile_pool(name="const", bufs=1))
         resident = ctx.enter_context(tc.tile_pool(name="resident", bufs=NBLK))
-        small = ctx.enter_context(tc.tile_pool(name="small", bufs=2))
+        small = ctx.enter_context(tc.tile_pool(name="small", bufs=4))
         work = ctx.enter_context(tc.tile_pool(name="work", bufs=4))
-        codes = ctx.enter_context(tc.tile_pool(name="codes", bufs=2))
-        psum = ctx.enter_context(tc.psum_pool(name="psum", bufs=2))
+        codes = ctx.enter_context(tc.tile_pool(name="codes", bufs=3))
+        psum = ctx.enter_context(tc.psum_pool(name="psum", bufs=1))
         ctx.enter_context(tc.manual_schedule())
 
         hx = []
@@ -82,7 +80,7 @@ def tile_decoder_pb_kernel(tc, h7_pre, g7, be7, W8, b8, out):
         nc.vector.memset(warm[:], 0.0)
         nc.scalar.activation(out=warm[:], in_=warm[:], func=ACT.Sigmoid)
 
-        gb_t = psum.tile([P, 512], F32, name="gb_t", tag="wt", bufs=1)
+        gb_t = psum.tile([P, 512], F32, name="gb_t", tag="wt")
         nc.tensor.transpose(gb_t[:, 0:P], gb_raw[:].bitcast(F32), ident[:])
         gb = const.tile([P, 256], F32)
         nc.vector.tensor_copy(out=gb[:], in_=gb_t[:, 0:P].bitcast(BF16))
@@ -91,6 +89,7 @@ def tile_decoder_pb_kernel(tc, h7_pre, g7, be7, W8, b8, out):
         sc = const.tile([P, NBLK * 16], F32)
         bi = const.tile([P, NBLK * 16], F32)
         out_v = out.rearrange("(t n) p c -> n t p c", t=2)
+        live = {}
 
         def transposes(bank, src, g):
             words = src[:].bitcast(F32)
@@ -102,178 +101,180 @@ def tile_decoder_pb_kernel(tc, h7_pre, g7, be7, W8, b8, out):
                         ident[:],
                     )
 
-        def chain_pool(j):
+        def unit_stats(j):
             w = 4 * UNIT
-            stp = st[:, j * 3 * w : (j + 1) * 3 * w].rearrange("q (c s) -> q c s", s=3)
+            return st[:, j * 3 * w : (j + 1) * 3 * w].rearrange("q (c s) -> q c s", s=3)
+
+        def rstd_on_pool(j):
+            w = 4 * UNIT
             var = small.tile([P, w], F32, name="var", tag="var")
             nc.gpsimd.tensor_scalar(
-                out=var[:], in0=stp[:, :, 2], scalar1=1.0 / ROWS, scalar2=EPS, op0=ALU.mult, op1=ALU.add
+                out=var[:], in0=unit_stats(j)[:, :, 2], scalar1=1.0 / ROWS, scalar2=EPS, op0=ALU.mult, op1=ALU.add
             )
-            rstd = small.tile([P, w], F32, name="rstd", tag="rstd", bufs=4)
-            tiles[("rstd", j)] = rstd
+            rstd = small.tile([P, w], F32, name="rstd", tag="rstd")
+            live[("rstd", j)] = rstd
             nc.gpsimd.tensor_tensor(out=rstd[:], in0=var[:], in1=neg_half[:], op=ALU.pow)
 
-        def chain_vector(j, part):
+        def scale_and_shift(j, part):
             w = 4 * UNIT
-            stp = st[:, j * 3 * w : (j + 1) * 3 * w].rearrange("q (c s) -> q c s", s=3)
             cols = slice(j * w, (j + 1) * w)
             if part == 0:
-                nc.vector.tensor_tensor(out=sc[:, cols], in0=tiles[("rstd", j)][:], in1=gb[:, cols], op=ALU.mult)
+                nc.vector.tensor_tensor(out=sc[:, cols], in0=live[("rstd", j)][:], in1=gb[:, cols], op=ALU.mult)
             elif part == 1:
                 ms = small.tile([P, w], F32, name="ms", tag="ms")
-                tiles[("ms", j)] = ms
-                nc.vector.tensor_tensor(out=ms[:], in0=stp[:, :, 1], in1=sc[:, cols], op=ALU.mult)
+                live[("ms", j)] = ms
+                nc.vector.tensor_tensor(out=ms[:], in0=unit_stats(j)[:, :, 1], in1=sc[:, cols], op=ALU.mult)
             else:
                 nc.vector.tensor_tensor(
-                    out=bi[:, cols], in0=gb[:, 128 + j * w : 128 + (j + 1) * w], in1=tiles[("ms", j)][:], op=ALU.subtract
+                    out=bi[:, cols], in0=gb[:, 128 + j * w : 128 + (j + 1) * w], in1=live[("ms", j)][:], op=ALU.subtract
                 )
 
-        banks = {}
-        tiles = {}
-
-        def regroup(s):
-            planes = tiles[("planes", s)]
-            grouped = work.tile([P, 4 * ROWS], BF16, name="grouped", tag="grouped", align_bytes=64)
-            tiles[("grouped", s)] = grouped
-            eng = regroup_engine(s)
-            dst = grouped[:].rearrange("q (c i j) -> q c j i", i=4, j=4)
-            src = planes[:].rearrange("q (j c i) -> q c j i", i=4, j=4)
-            if eng == "v":
-                nc.vector.tensor_copy(out=dst, in_=src)
-            elif eng == "s":
-                nc.scalar.copy(out=dst, in_=src)
-            else:
-                nc.gpsimd.tensor_scalar(out=dst, in0=src, scalar1=1.0, scalar2=0.0, op0=ALU.mult, op1=ALU.add)
-
-        def product(p):
-            ac, asc = tiles[("ac", p)]
-            wc, ws = tiles[("wc", p)]
-            acc = psum.tile([P, 512], F32, name="acc", tag="acc", bufs=1)
-            banks[("acc", p)] = acc
-            for t in range(2):
-                for g in range(PASSES):
-                    a_cols = slice(g * ROWS + t * P, g * ROWS + (t + 1) * P)
-                    w_cols = slice(g * CH, (g + 1) * CH)
-                    nc.tensor.matmul_mx(
-                        out=acc[:, t * CH : (t + 1) * CH],
-                        lhsT=ac[:, a_cols].bitcast(FP8X4),
-                        lhsT_scale=asc[:, a_cols],
-                        rhs=wc[:, w_cols].bitcast(FP8X4),
-                        rhs_scale=ws[:, w_cols],
-                        start=(g == 0),
-                        stop=(g == PASSES - 1),
+        def norm(s):
+            bank = live[("hb", s)][:].bitcast(BF16).rearrange("q (u n e) -> q u n e", u=2, e=2)
+            planes = work.tile([P, 4 * ROWS], BF16, name="planes", tag="planes")
+            live[("planes", s)] = planes
+            for u in range(2):
+                for e in range(2):
+                    col = (2 * s + u) * 2 + e
+                    j = 2 * u + e
+                    nc.scalar.activation(
+                        out=planes[:, j * ROWS : (j + 1) * ROWS],
+                        in_=bank[:, u, :, e],
+                        func=ACT.Relu,
+                        bias=bi[:, col : col + 1],
+                        scale=sc[:, col : col + 1],
                     )
 
+        def regroup(s):
+            grouped = work.tile([P, 4 * ROWS], BF16, name="grouped", tag="grouped", align_bytes=64)
+            live[("grouped", s)] = grouped
+            dst = grouped[:].rearrange("q (c i j) -> q c j i", i=4, j=4)
+            src = live[("planes", s)][:].rearrange("q (j c i) -> q c j i", i=4, j=4)
+            if regroup_on_scalar(s):
+                nc.scalar.copy(out=dst, in_=src)
+            else:
+                nc.vector.tensor_copy(out=dst, in_=src)
+
+        def quantise(kind, s, width):
+            p, g = s // PASSES, s % PASSES
+            if g == 0:
+                words = codes.tile([P, PASSES * width], U32, name="words", tag=kind + "_words", align_bytes=64)
+                scales = codes.tile([P, PASSES * width], U8, name="scales", tag=kind + "_scales", align_bytes=64)
+                live[(kind, p)] = (words, scales)
+            words, scales = live[(kind, p)]
+            nc.vector.quantize_mx(
+                out=words[:, g * width : (g + 1) * width].bitcast(FP8X4),
+                scales=scales[:, g * width : (g + 1) * width],
+                in_=live[("grouped" if kind == "a" else "wg", s)][:],
+            )
+
+        def mx_pass(acc_cols, p, g, t):
+            a_words, a_scales = live[("a", p)]
+            w_words, w_scales = live[("w", p)]
+            a_cols = slice(g * ROWS + t * P, g * ROWS + (t + 1) * P)
+            w_cols = slice(g * CH, (g + 1) * CH)
+            nc.tensor.matmul_mx(
+                out=acc_cols,
+                lhsT=a_words[:, a_cols].bitcast(FP8X4),
+                lhsT_scale=a_scales[:, a_cols],
+                rhs=w_words[:, w_cols].bitcast(FP8X4),
+                rhs_scale=w_scales[:, w_cols],
+                start=(g == 0),
+                stop=(g == PASSES - 1),
+            )
+
+        def product(p):
+            acc = psum.tile([P, 512], F32, name="acc", tag="acc")
+            live[("acc", p)] = acc
+            for t in range(2):
+                for g in range(PASSES):
+                    mx_pass(acc[:, t * CH : (t + 1) * CH], p, g, t)
+
         def add_bias(p):
-            acc = banks[("acc", p)]
             y = work.tile([P, 2 * CH], F32, name="y", tag="y")
-            tiles[("y", p)] = y
+            live[("y", p)] = y
             nc.vector.tensor_tensor(
                 out=y[:].rearrange("n (t c) -> n t c", t=2),
-                in0=acc[:].rearrange("n (t c) -> n t c", t=2),
+                in0=live[("acc", p)][:].rearrange("n (t c) -> n t c", t=2),
                 in1=bb[:, p * CH : (p + 1) * CH].unsqueeze(1).to_broadcast([P, 2, CH]),
                 op=ALU.add,
             )
 
         def sigmoid_store(p):
-            y = tiles[("y", p)]
             o = work.tile([P, 2 * CH], F32, name="o", tag="o")
-            nc.scalar.activation(out=o[:], in_=y[:], func=ACT.Sigmoid)
+            nc.scalar.activation(out=o[:], in_=live[("y", p)][:], func=ACT.Sigmoid)
             nc.sync.dma_start(out=out_v[:, :, p, :], in_=o[:].rearrange("n (t c) -> n t c", t=2))
 
+        last = NBLK - 1
         mx_at = {}
         add_at = {}
         sig_at = {}
-        for tau in range(STEPS + D_B + 8):
-            s_a, s_w, s_b = tau, tau - D_W, tau - D_B
-            if s_a < STEPS:
-                hb = psum.tile([P, 512], F32, name="hb", tag="hb", bufs=6)
-                banks[("hb", s_a)] = hb
-                transposes(hb, hx[s_a // PASSES], s_a % PASSES)
+        for tau in range(STEPS + LAG_NORM + 3):
+            s_h, s_w, s_n = tau, tau - LAG_W, tau - LAG_NORM
+            if s_h < STEPS:
+                hb = psum.tile([P, 512], F32, name="hb", tag="hb", bufs=H_BANKS)
+                live[("hb", s_h)] = hb
+                transposes(hb, hx[s_h // PASSES], s_h % PASSES)
             if 0 <= s_w < STEPS:
-                wt = psum.tile([P, 512], F32, name="wt", tag="wt", bufs=1)
-                banks[("wt", s_w)] = wt
+                wt = psum.tile([P, 512], F32, name="wt", tag="wt")
+                live[("wt", s_w)] = wt
                 transposes(wt, wx[s_w // PASSES], s_w % PASSES)
             if tau in mx_at:
                 product(mx_at[tau])
             if tau in add_at:
                 add_bias(add_at[tau])
-            j_c = (tau - D_C - (UNIT - 1)) // UNIT if (tau - D_C - (UNIT - 1)) % UNIT == 0 else -1
-            do_chain = 0 <= j_c < STEPS // UNIT
-            if do_chain:
-                chain_vector(j_c, 0)
-            if s_a < STEPS:
-                hab = banks[("hb", s_a)][:].bitcast(BF16)
-                nc.vector.bn_stats(out=st[:, 2 * s_a * 6 : (2 * s_a + 1) * 6], in_=hab[:, 0:512])
-            if do_chain:
-                chain_vector(j_c, 1)
-            if s_a < STEPS:
-                nc.vector.bn_stats(out=st[:, (2 * s_a + 1) * 6 : (2 * s_a + 2) * 6], in_=hab[:, 512:1024])
-                if s_a % UNIT == UNIT - 1:
-                    chain_pool(s_a // UNIT)
-            if do_chain:
-                chain_vector(j_c, 2)
+            j_c = tau - LAG_CHAIN - (UNIT - 1)
+            chain_now = j_c >= 0 and j_c % UNIT == 0 and j_c // UNIT < N_UNITS
+            j_c = j_c // UNIT
+            if chain_now:
+                scale_and_shift(j_c, 0)
+            if s_h < STEPS:
+                hab = live[("hb", s_h)][:].bitcast(BF16)
+                nc.vector.bn_stats(out=st[:, 2 * s_h * 6 : (2 * s_h + 1) * 6], in_=hab[:, 0:512])
+            if chain_now:
+                scale_and_shift(j_c, 1)
+            if s_h < STEPS:
+                nc.vector.bn_stats(out=st[:, (2 * s_h + 1) * 6 : (2 * s_h + 2) * 6], in_=hab[:, 512:1024])
+                if s_h % UNIT == UNIT - 1:
+                    rstd_on_pool(s_h // UNIT)
+            if chain_now:
+                scale_and_shift(j_c, 2)
             if tau in sig_at:
                 sigmoid_store(sig_at[tau])
-            if 0 <= s_b < STEPS:
-                hbb = banks[("hb", s_b)][:].bitcast(BF16).rearrange("q (u n e) -> q u n e", u=2, e=2)
-                planes = work.tile([P, 4 * ROWS], BF16, name="planes", tag="planes")
-                tiles[("planes", s_b)] = planes
-                for u in range(2):
-                    for e in range(2):
-                        col = (2 * s_b + u) * 2 + e
-                        j = 2 * u + e
-                        nc.scalar.activation(
-                            out=planes[:, j * ROWS : (j + 1) * ROWS],
-                            in_=hbb[:, u, :, e],
-                            func=ACT.Relu,
-                            bias=bi[:, col : col + 1],
-                            scale=sc[:, col : col + 1],
-                        )
+            if 0 <= s_n < STEPS:
+                norm(s_n)
             if 0 <= s_w < STEPS:
                 wg = work.tile([P, 4 * CH], BF16, name="wg", tag="wg", align_bytes=64)
-                tiles[("wg", s_w)] = wg
-                wg_dst = wg[:].bitcast(F32).rearrange("q (c u) -> q c u", u=2)
-                wt_src = banks[("wt", s_w)][:].rearrange("q (u c) -> q c u", u=2)
-                if weights_copy_on_vector(s_w):
-                    nc.vector.tensor_copy(out=wg_dst, in_=wt_src)
-                else:
-                    nc.scalar.copy(out=wg_dst, in_=wt_src)
-            s_q = s_w - 1
+                live[("wg", s_w)] = wg
+                nc.scalar.copy(
+                    out=wg[:].bitcast(F32).rearrange("q (c u) -> q c u", u=2),
+                    in_=live[("wt", s_w)][:].rearrange("q (u c) -> q c u", u=2),
+                )
+            if 0 <= s_w - 1 < STEPS:
+                quantise("w", s_w - 1, CH)
+            s_q = s_n - 2
+            if 0 <= s_q < STEPS:
+                quantise("a", s_q, ROWS)
+            if 0 <= s_n - 1 < STEPS:
+                regroup(s_n - 1)
             if 0 <= s_q < STEPS:
                 p, g = s_q // PASSES, s_q % PASSES
-                if g == 0:
-                    wc = codes.tile([P, PASSES * CH], U32, name="wc", tag="wc", align_bytes=64)
-                    ws = codes.tile([P, PASSES * CH], U8, name="ws", tag="ws", align_bytes=64)
-                    tiles[("wc", p)] = (wc, ws)
-                wc, ws = tiles[("wc", p)]
-                nc.vector.quantize_mx(
-                    out=wc[:, g * CH : (g + 1) * CH].bitcast(FP8X4),
-                    scales=ws[:, g * CH : (g + 1) * CH],
-                    in_=tiles[("wg", s_q)][:],
-                )
-            s_q = s_b - 2
-            if 0 <= s_q < STEPS:
-                p, g = s_q // PASSES, s_q % PASSES
-                if g == 0:
-                    ac = codes.tile([P, PASSES * ROWS], U32, name="ac", tag="ac", align_bytes=64)
-                    asc = codes.tile([P, PASSES * ROWS], U8, name="asc", tag="asc", align_bytes=64)
-                    tiles[("ac", p)] = (ac, asc)
-                ac, asc = tiles[("ac", p)]
-                nc.vector.quantize_mx(
-                    out=ac[:, g * ROWS : (g + 1) * ROWS].bitcast(FP8X4),
-                    scales=asc[:, g * ROWS : (g + 1) * ROWS],
-                    in_=tiles[("grouped", s_q)][:],
-                )
-            if 0 <= s_b - 1 < STEPS:
-                regroup(s_b - 1)
-            if 0 <= s_q < STEPS and s_q % PASSES == PASSES - 1:
-                p = s_q // PASSES
-                if p == NBLK - 1:
-                    product(p)
-                    add_bias(p)
-                    sigmoid_store(p)
-                else:
-                    mx_at[tau + D_MX] = p
-                    add_at[tau + D_MX + 1] = p
-                    sig_at[tau + D_MX + 2] = p
+                if p == last:
+                    if g == 0:
+                        for t in range(2):
+                            acc_t = psum.tile([P, 512], F32, name="acc_t", tag="hb", bufs=H_BANKS)
+                            live[("acc_t", t)] = acc_t
+                    for t in range(2):
+                        mx_pass(live[("acc_t", t)][:, 0:CH], p, g, t)
+                elif g == PASSES - 1:
+                    mx_at[tau + LAG_MX] = p
+                    add_at[tau + LAG_MX + 1] = p
+                    sig_at[tau + LAG_MX + 2] = p
+        for t in range(2):
+            y_t = work.tile([P, CH], F32, name="y_t", tag="y_t", bufs=2)
+            nc.vector.tensor_tensor(
+                out=y_t[:], in0=live[("acc_t", t)][:, 0:CH], in1=bb[:, last * CH : (last + 1) * CH], op=ALU.add
+            )
+            o_t = work.tile([P, CH], F32, name="o_t", tag="o_t", bufs=2)
+            nc.scalar.activation(out=o_t[:], in_=y_t[:], func=ACT.Sigmoid)
+            nc.sync.dma_start(out=out_v[:, t, last, :], in_=o_t[:])

@@ -40,7 +40,6 @@ def tile_decoder_pb_kernel(tc, h7_pre, g7, be7, W8, b8, out):
         work = ctx.enter_context(tc.tile_pool(name="work", bufs=4))
         codes = ctx.enter_context(tc.tile_pool(name="codes", bufs=3))
         psum = ctx.enter_context(tc.psum_pool(name="psum", bufs=1))
-        ctx.enter_context(tc.manual_schedule())
 
         hx = []
         wx = []

from contextlib import ExitStack

import concourse.mybir as mybir
from concourse.masks import make_identity

F32 = mybir.dt.float32
BF16 = mybir.dt.bfloat16
U32 = mybir.dt.uint32
U8 = mybir.dt.uint8
FP8X4 = mybir.dt.float8_e4m3fn_x4
ALU = mybir.AluOpType
ACT = mybir.ActivationFunctionType

NBLK, ROWS, K, CH = 8, 256, 2048, 256
EPS = 1e-5
P = 128
PASSES = K // 512
STEPS = NBLK * PASSES
FLOPS = 2 * NBLK * ROWS * CH * K

UNIT = 2
N_UNITS = STEPS // UNIT
LAG_W = 1
LAG_CHAIN = 3
LAG_NORM = 5
LAG_MX = 2
H_BANKS = 6


def regroup_on_scalar(s):
    return s % 3 == 2 and s < 24


def tile_decoder_pb_kernel(tc, h7_pre, g7, be7, W8, b8, out):
    nc = tc.nc
    with ExitStack() as ctx:
        const = ctx.enter_context(tc.tile_pool(name="const", bufs=1))
        resident = ctx.enter_context(tc.tile_pool(name="resident", bufs=NBLK))
        small = ctx.enter_context(tc.tile_pool(name="small", bufs=4))
        work = ctx.enter_context(tc.tile_pool(name="work", bufs=4))
        codes = ctx.enter_context(tc.tile_pool(name="codes", bufs=3))
        psum = ctx.enter_context(tc.psum_pool(name="psum", bufs=1))

        hx = []
        wx = []
        for p in range(NBLK):
            hx_p = resident.tile([P, 2 * K], BF16, name="hx_p", tag="hx")
            wx_p = resident.tile([P, 2 * K], BF16, name="wx_p", tag="wx")
            hx.append(hx_p)
            wx.append(wx_p)

        def load(dst, src, k0, k1):
            nc.sync.dma_start(
                out=dst[:].rearrange("n (t k) -> n t k", t=2)[:, :, k0:k1],
                in_=src.rearrange("(t n) k -> n t k", t=2)[:, :, k0:k1],
            )

        gb_raw = const.tile([P, 256], BF16)
        nc.scalar.dma_start(out=gb_raw[0:64, :], in_=g7.rearrange("p (r k) -> (p r) k", k=256))
        nc.scalar.dma_start(out=gb_raw[64:128, :], in_=be7.rearrange("p (r k) -> (p r) k", k=256))
        bb = const.tile([P, NBLK * CH], BF16)

        load(hx[0], h7_pre[0], 0, 512)
        load(hx[0], h7_pre[0], 512, 1024)
        load(wx[0], W8[0], 0, 1024)
        load(hx[0], h7_pre[0], 1024, 2048)
        load(wx[0], W8[0], 1024, 2048)
        for p in range(1, NBLK):
            load(hx[p], h7_pre[p], 0, K)
            load(wx[p], W8[p], 0, K)
            if p == 1:
                nc.sync.dma_start(out=bb[:], in_=b8.rearrange("p c -> (p c)").partition_broadcast(P))

        ident = const.tile([P, P], F32)
        make_identity(nc, ident[:])
        neg_half = const.tile([P, 4 * UNIT], F32)
        nc.gpsimd.memset(neg_half[:], -0.5)
        warm = const.tile([P, 1], F32)
        nc.vector.memset(warm[:], 0.0)
        nc.scalar.activation(out=warm[:], in_=warm[:], func=ACT.Sigmoid)

        gb_t = psum.tile([P, 512], F32, name="gb_t", tag="wt")
        nc.tensor.transpose(gb_t[:, 0:P], gb_raw[:].bitcast(F32), ident[:])
        gb = const.tile([P, 256], F32)
        nc.vector.tensor_copy(out=gb[:], in_=gb_t[:, 0:P].bitcast(BF16))

        st = const.tile([P, NBLK * 8 * 6], F32)
        sc = const.tile([P, NBLK * 16], F32)
        bi = const.tile([P, NBLK * 16], F32)
        out_v = out.rearrange("(t n) p c -> n t p c", t=2)
        live = {}

        def transposes(bank, src, g):
            words = src[:].bitcast(F32)
            for u in range(2):
                for t in range(2):
                    nc.tensor.transpose(
                        bank[:, u * 256 + t * P : u * 256 + (t + 1) * P],
                        words[:, t * 1024 + (2 * g + u) * P : t * 1024 + (2 * g + u + 1) * P],
                        ident[:],
                    )

        def unit_stats(j):
            w = 4 * UNIT
            return st[:, j * 3 * w : (j + 1) * 3 * w].rearrange("q (c s) -> q c s", s=3)

        def rstd_on_pool(j):
            w = 4 * UNIT
            var = small.tile([P, w], F32, name="var", tag="var")
            nc.gpsimd.tensor_scalar(
                out=var[:], in0=unit_stats(j)[:, :, 2], scalar1=1.0 / ROWS, scalar2=EPS, op0=ALU.mult, op1=ALU.add
            )
            rstd = small.tile([P, w], F32, name="rstd", tag="rstd")
            live[("rstd", j)] = rstd
            nc.gpsimd.tensor_tensor(out=rstd[:], in0=var[:], in1=neg_half[:], op=ALU.pow)

        def scale_and_shift(j, part):
            w = 4 * UNIT
            cols = slice(j * w, (j + 1) * w)
            if part == 0:
                nc.vector.tensor_tensor(out=sc[:, cols], in0=live[("rstd", j)][:], in1=gb[:, cols], op=ALU.mult)
            elif part == 1:
                ms = small.tile([P, w], F32, name="ms", tag="ms")
                live[("ms", j)] = ms
                nc.vector.tensor_tensor(out=ms[:], in0=unit_stats(j)[:, :, 1], in1=sc[:, cols], op=ALU.mult)
            else:
                nc.vector.tensor_tensor(
                    out=bi[:, cols], in0=gb[:, 128 + j * w : 128 + (j + 1) * w], in1=live[("ms", j)][:], op=ALU.subtract
                )

        def norm(s):
            bank = live[("hb", s)][:].bitcast(BF16).rearrange("q (u n e) -> q u n e", u=2, e=2)
            planes = work.tile([P, 4 * ROWS], BF16, name="planes", tag="planes")
            live[("planes", s)] = planes
            for u in range(2):
                for e in range(2):
                    col = (2 * s + u) * 2 + e
                    j = 2 * u + e
                    nc.scalar.activation(
                        out=planes[:, j * ROWS : (j + 1) * ROWS],
                        in_=bank[:, u, :, e],
                        func=ACT.Relu,
                        bias=bi[:, col : col + 1],
                        scale=sc[:, col : col + 1],
                    )

        def regroup(s):
            grouped = work.tile([P, 4 * ROWS], BF16, name="grouped", tag="grouped", align_bytes=64)
            live[("grouped", s)] = grouped
            dst = grouped[:].rearrange("q (c i j) -> q c j i", i=4, j=4)
            src = live[("planes", s)][:].rearrange("q (j c i) -> q c j i", i=4, j=4)
            if regroup_on_scalar(s):
                nc.scalar.copy(out=dst, in_=src)
            else:
                nc.vector.tensor_copy(out=dst, in_=src)

        def quantise(kind, s, width):
            p, g = s // PASSES, s % PASSES
            if g == 0:
                words = codes.tile([P, PASSES * width], U32, name="words", tag=kind + "_words", align_bytes=64)
                scales = codes.tile([P, PASSES * width], U8, name="scales", tag=kind + "_scales", align_bytes=64)
                live[(kind, p)] = (words, scales)
            words, scales = live[(kind, p)]
            nc.vector.quantize_mx(
                out=words[:, g * width : (g + 1) * width].bitcast(FP8X4),
                scales=scales[:, g * width : (g + 1) * width],
                in_=live[("grouped" if kind == "a" else "wg", s)][:],
            )

        def mx_pass(acc_cols, p, g, t):
            a_words, a_scales = live[("a", p)]
            w_words, w_scales = live[("w", p)]
            a_cols = slice(g * ROWS + t * P, g * ROWS + (t + 1) * P)
            w_cols = slice(g * CH, (g + 1) * CH)
            nc.tensor.matmul_mx(
                out=acc_cols,
                lhsT=a_words[:, a_cols].bitcast(FP8X4),
                lhsT_scale=a_scales[:, a_cols],
                rhs=w_words[:, w_cols].bitcast(FP8X4),
                rhs_scale=w_scales[:, w_cols],
                start=(g == 0),
                stop=(g == PASSES - 1),
            )

        def product(p):
            acc = psum.tile([P, 512], F32, name="acc", tag="acc")
            live[("acc", p)] = acc
            for t in range(2):
                for g in range(PASSES):
                    mx_pass(acc[:, t * CH : (t + 1) * CH], p, g, t)

        def add_bias(p):
            y = work.tile([P, 2 * CH], F32, name="y", tag="y")
            live[("y", p)] = y
            nc.vector.tensor_tensor(
                out=y[:].rearrange("n (t c) -> n t c", t=2),
                in0=live[("acc", p)][:].rearrange("n (t c) -> n t c", t=2),
                in1=bb[:, p * CH : (p + 1) * CH].unsqueeze(1).to_broadcast([P, 2, CH]),
                op=ALU.add,
            )

        def sigmoid_store(p):
            o = work.tile([P, 2 * CH], F32, name="o", tag="o")
            nc.scalar.activation(out=o[:], in_=live[("y", p)][:], func=ACT.Sigmoid)
            nc.sync.dma_start(out=out_v[:, :, p, :], in_=o[:].rearrange("n (t c) -> n t c", t=2))

        last = NBLK - 1
        mx_at = {}
        add_at = {}
        sig_at = {}
        for tau in range(STEPS + LAG_NORM + 3):
            s_h, s_w, s_n = tau, tau - LAG_W, tau - LAG_NORM
            if s_h < STEPS:
                hb = psum.tile([P, 512], F32, name="hb", tag="hb", bufs=H_BANKS)
                live[("hb", s_h)] = hb
                transposes(hb, hx[s_h // PASSES], s_h % PASSES)
            if 0 <= s_w < STEPS:
                wt = psum.tile([P, 512], F32, name="wt", tag="wt")
                live[("wt", s_w)] = wt
                transposes(wt, wx[s_w // PASSES], s_w % PASSES)
            if tau in mx_at:
                product(mx_at[tau])
            if tau in add_at:
                add_bias(add_at[tau])
            j_c = tau - LAG_CHAIN - (UNIT - 1)
            chain_now = j_c >= 0 and j_c % UNIT == 0 and j_c // UNIT < N_UNITS
            j_c = j_c // UNIT
            if chain_now:
                scale_and_shift(j_c, 0)
            if s_h < STEPS:
                hab = live[("hb", s_h)][:].bitcast(BF16)
                nc.vector.bn_stats(out=st[:, 2 * s_h * 6 : (2 * s_h + 1) * 6], in_=hab[:, 0:512])
            if chain_now:
                scale_and_shift(j_c, 1)
            if s_h < STEPS:
                nc.vector.bn_stats(out=st[:, (2 * s_h + 1) * 6 : (2 * s_h + 2) * 6], in_=hab[:, 512:1024])
                if s_h % UNIT == UNIT - 1:
                    rstd_on_pool(s_h // UNIT)
            if chain_now:
                scale_and_shift(j_c, 2)
            if tau in sig_at:
                sigmoid_store(sig_at[tau])
            if 0 <= s_n < STEPS:
                norm(s_n)
            if 0 <= s_w < STEPS:
                wg = work.tile([P, 4 * CH], BF16, name="wg", tag="wg", align_bytes=64)
                live[("wg", s_w)] = wg
                nc.scalar.copy(
                    out=wg[:].bitcast(F32).rearrange("q (c u) -> q c u", u=2),
                    in_=live[("wt", s_w)][:].rearrange("q (u c) -> q c u", u=2),
                )
            if 0 <= s_w - 1 < STEPS:
                quantise("w", s_w - 1, CH)
            s_q = s_n - 2
            if 0 <= s_q < STEPS:
                quantise("a", s_q, ROWS)
            if 0 <= s_n - 1 < STEPS:
                regroup(s_n - 1)
            if 0 <= s_q < STEPS:
                p, g = s_q // PASSES, s_q % PASSES
                if p == last:
                    if g == 0:
                        for t in range(2):
                            acc_t = psum.tile([P, 512], F32, name="acc_t", tag="hb", bufs=H_BANKS)
                            live[("acc_t", t)] = acc_t
                    for t in range(2):
                        mx_pass(live[("acc_t", t)][:, 0:CH], p, g, t)
                elif g == PASSES - 1:
                    mx_at[tau + LAG_MX] = p
                    add_at[tau + LAG_MX + 1] = p
                    sig_at[tau + LAG_MX + 2] = p
        for t in range(2):
            y_t = work.tile([P, CH], F32, name="y_t", tag="y_t", bufs=2)
            nc.vector.tensor_tensor(
                out=y_t[:], in0=live[("acc_t", t)][:, 0:CH], in1=bb[:, last * CH : (last + 1) * CH], op=ALU.add
            )
            o_t = work.tile([P, CH], F32, name="o_t", tag="o_t", bufs=2)
            nc.scalar.activation(out=o_t[:], in_=y_t[:], func=ACT.Sigmoid)
            nc.sync.dma_start(out=out_v[:, t, last, :], in_=o_t[:])
